import numpy as np
import ml_dtypes


def mxq(x, axis, fmt="e4m3"):
    dtype, down = {"e4m3": (ml_dtypes.float8_e4m3fn, 7), "e5m2": (ml_dtypes.float8_e5m2, 14)}[fmt]
    v = np.moveaxis(np.asarray(x, np.float32).astype(ml_dtypes.bfloat16).astype(np.float64), axis, -1)
    blocks = v.reshape(v.shape[:-1] + (-1, 32))
    amax = np.abs(blocks).max(-1, keepdims=True)
    byte = np.maximum(np.where(amax > 0, np.frexp(amax)[1] - 1 + 127, 0) - down, 1)
    scale = np.exp2(byte - 127.0)
    codes = (blocks / scale).astype(np.float32).astype(dtype).astype(np.float64)
    return np.moveaxis((codes * scale).reshape(v.shape), -1, axis)


WIDE = False


def mx_kscale(k):
    if not WIDE:
        return np.ones(k)
    levels = np.array([10, -10, 5, -5, 0])
    a = np.random.permutation(np.resize(levels, k // 512 * 4)).reshape(k // 512, 4)
    idx = np.arange(k)
    return np.exp2(a[idx // 512, idx % 128 // 32])


BF16 = ml_dtypes.bfloat16


def bf(x):
    return np.asarray(x, np.float32).astype(BF16)


def f64(x):
    return np.asarray(x).astype(np.float64)


E2M1 = np.array([0.0, 0.5, 1.0, 1.5, 2.0, 3.0, 4.0, 6.0, -0.0, -0.5, -1.0, -1.5, -2.0, -3.0, -4.0, -6.0])


def pack_weight(w, fmt):
    k, n = w.shape
    w = f64(bf(w)).reshape(k // 32, 32, n)
    amax = np.abs(w).max(1)
    if fmt == "e4m3":
        byte = np.frexp(amax)[1] - 1 + 127 - 7
    else:
        mant, ex = np.frexp(amax / 6.0)
        byte = np.where(mant > 0.5, ex, ex - 1) + 127
    byte = np.clip(np.where(amax > 0, byte, 1), 1, 254)
    scaled = (w * np.exp2(127.0 - byte)[:, None, :]).reshape(k, n).astype(np.float32)
    by_word = np.ascontiguousarray(scaled.reshape(k // 512, 128, 4, n).transpose(0, 1, 3, 2))
    if fmt == "e4m3":
        words = by_word.astype(ml_dtypes.float8_e4m3fn).view(np.uint8)
    else:
        c = by_word.astype(ml_dtypes.float4_e2m1fn).view(np.uint8) & 0xF
        words = c[..., 0::2] | (c[..., 1::2] << 4)
    return np.ascontiguousarray(words), np.ascontiguousarray(byte.astype(np.uint8).reshape(k // 512, 16, n))


def unpack_weight(words, scales, fmt):
    g, p, n, _ = words.shape
    if fmt == "e4m3":
        vals = np.ascontiguousarray(words).view(ml_dtypes.float8_e4m3fn).astype(np.float64)
    else:
        nib = np.empty((g, p, n, 4), np.uint8)
        nib[..., 0::2] = words & 0xF
        nib[..., 1::2] = words >> 4
        vals = E2M1[nib]
    vals = vals * np.repeat(np.exp2(scales.astype(np.float64) - 127.0), 8, axis=1)[..., None]
    return vals.transpose(0, 1, 3, 2).reshape(g * 512, n)


B, S, K, N = 2, 64, 4096, 4096
FMT = "e4m3"


def setup_inputs():
    s = mx_kscale(K)
    input = bf(np.random.standard_normal((B, S, K)) * s)
    weight = np.random.standard_normal((N, K)) / np.sqrt(K) / s[None, :]
    words, scales = pack_weight(np.ascontiguousarray(weight.T), FMT)
    bias = bf(np.random.standard_normal(N) * 0.5)
    return {"input": input,
            "weight_words": words,
            "weight_scales": scales,
            "bias": bias}


def reference(input, weight_words, weight_scales, bias):
    xq = mxq(f64(input), 2, "e4m3")
    wq = unpack_weight(weight_words, weight_scales, FMT)
    out = xq.reshape(B * S, K) @ wq
    return out.reshape(B, S, N) + f64(bias)

@@ -1,0 +1,152 @@
+from contextlib import ExitStack
+
+import concourse.mybir as mybir
+from concourse.masks import make_identity
+
+F32 = mybir.dt.float32
+BF16 = mybir.dt.bfloat16
+U32 = mybir.dt.uint32
+U8 = mybir.dt.uint8
+I32 = mybir.dt.int32
+FP8X4 = mybir.dt.float8_e4m3fn_x4
+
+P = 128
+K = 4096
+N = 4096
+K_PASS = 512
+GROUPS = K // K_PASS
+BANK = 512
+N_BANKS = N // BANK
+FLOPS = 2 * P * K * N
+
+G_FULL = 5
+TAIL_RANGES = ((0, 2048, 1), (2048, 3072, 3), (3072, 3584, 3), (3584, 4096, 3))
+SCALES_ON_GPSIMD = False
+
+
+def load_plan():
+    plan = [(g, g + 1, 0, N) for g in range(G_FULL)]
+    for c0, c1, step in TAIL_RANGES:
+        for g in range(G_FULL, GROUPS, step):
+            plan.append((g, min(g + step, GROUPS), c0, c1))
+    return plan
+
+
+def tile_tiledlinear_w_kernel(tc, x_in, weight_words, weight_scales, bias, out):
+    nc = tc.nc
+    x_rows = x_in.flatten_outer_dims()
+    out_rows = out.flatten_outer_dims()
+    plan = load_plan()
+    with ExitStack() as stack:
+        keep = stack.enter_context(tc.tile_pool(name="keep", bufs=1))
+        banks = stack.enter_context(tc.psum_pool(name="banks", bufs=1))
+        stack.enter_context(tc.manual_schedule())
+
+        x_sb = keep.tile([P, K], BF16, name="x_sb", align_bytes=64)
+        grouped = keep.tile([P, K], BF16, name="grouped", align_bytes=64)
+        x_codes = keep.tile([P, K // 4], U32, name="x_codes", align_bytes=64)
+        x_scales = keep.tile([P, K // 4], U8, name="x_scales", align_bytes=64)
+        planes = keep.tile([P, 2 * N], U8, name="planes", align_bytes=64)
+        ident = keep.tile([P, P], F32, name="ident")
+        ident_bf = keep.tile([P, N_BANKS], BF16, name="ident_bf")
+        bias_rows = keep.tile([P, BANK], BF16, name="bias_rows")
+        bias_all = keep.tile([P, N], F32, name="bias_all")
+
+        nc.sync.dma_start(out=x_sb[:], in_=x_rows)
+        nc.vector.memset(planes[:].bitcast(I32), 0)
+        nc.vector.memset(bias_rows[:], 0.0)
+        make_identity(nc, ident[:])
+        nc.scalar.dma_start(out=bias_rows[0:N_BANKS, :], in_=bias.rearrange("(c n) -> c n", c=N_BANKS))
+        nc.vector.tensor_copy(out=ident_bf[:], in_=ident[:, 0:N_BANKS])
+        for h in range(2):
+            for q in (0, 1, 2, 3):
+                dst = planes[32 * q : 32 * q + 16, h * N : (h + 1) * N]
+                src = weight_scales[4 * h : 4 * h + 4, 4 * q : 4 * q + 4, :]
+                if SCALES_ON_GPSIMD:
+                    nc.gpsimd.dma_start(out=dst.bitcast(F32), in_=src.bitcast(F32))
+                else:
+                    nc.sync.dma_start(out=dst.bitcast(I32), in_=src.bitcast(I32))
+        w_tiles = []
+        for i, (g0, g1, c0, c1) in enumerate(plan):
+            wt = keep.tile([P, g1 - g0, c1 - c0], U32, name="w%d" % i, align_bytes=64)
+            src = weight_words[g0:g1].rearrange("g p n t -> p g (n t)")[:, :, 4 * c0 : 4 * c1]
+            nc.sync.dma_start(out=wt[:].bitcast(I32), in_=src.bitcast(I32))
+            w_tiles.append(wt)
+
+        def bias_matmul(c):
+            bt = banks.tile([P, BANK], F32, name="bias_ps%d" % c, tag="bank%d" % (4 + c % 4))
+            nc.tensor.matmul(
+                out=bt[:],
+                lhsT=ident_bf[:, c : c + 1].to_broadcast([P, P]),
+                rhs=bias_rows[:],
+                start=True,
+                stop=True,
+            )
+            return bt
+
+        first = [bias_matmul(c) for c in range(4)]
+        for c in range(4):
+            nc.scalar.copy(out=bias_all[:, c * BANK : (c + 1) * BANK], in_=first[c][:])
+
+        x_words = x_sb[:].bitcast(F32)
+        grouped_words = grouped[:].bitcast(F32)
+        tps = []
+        for b in range(4):
+            tp = banks.tile([P, 2, 2, P], F32, name="tp%d" % b, tag="bank%d" % b)
+            for gi in range(2):
+                g = 2 * b + gi
+                for u in range(2):
+                    nc.tensor.transpose(
+                        out=tp[:, gi, u, :],
+                        in_=x_words[:, 256 * g + u : 256 * (g + 1) : 2],
+                        identity=ident[:],
+                    )
+            tps.append(tp)
+        for b in range(4):
+            dst = grouped_words[:, 512 * b : 512 * (b + 1)].rearrange("p (g r u) -> p g r u", g=2, u=2)
+            src = tps[b][:].rearrange("p g u r -> p g r u")
+            if b < 2:
+                nc.vector.tensor_copy(out=dst, in_=src)
+            else:
+                nc.scalar.copy(out=dst, in_=src)
+        for h in range(2):
+            nc.vector.quantize_mx(
+                out=x_codes[:, 512 * h : 512 * (h + 1)].bitcast(FP8X4),
+                scales=x_scales[:, 512 * h : 512 * (h + 1)],
+                in_=grouped[:, 2048 * h : 2048 * (h + 1)],
+            )
+        second = [bias_matmul(c) for c in range(4, 8)]
+        for c in range(4, 8):
+            dst = bias_all[:, c * BANK : (c + 1) * BANK]
+            if c % 2 == 0:
+                nc.scalar.copy(out=dst, in_=second[c - 4][:])
+            else:
+                nc.vector.tensor_copy(out=dst, in_=second[c - 4][:])
+
+        acc = {}
+        for i, (g0, g1, c0, c1) in enumerate(plan):
+            for g in range(g0, g1):
+                k_off = 4 * (g % 4)
+                col0 = (g // 4) * N
+                for b in range(c0 // BANK, c1 // BANK):
+                    if g == 0:
+                        acc[b] = banks.tile([P, BANK], F32, name="acc%d" % b, tag="bank%d" % b)
+                    nc.tensor.matmul_mx(
+                        out=acc[b][:],
+                        lhsT=x_codes[:, P * g : P * (g + 1)].bitcast(FP8X4),
+                        lhsT_scale=x_scales[:, P * g : P * (g + 1)],
+                        rhs=w_tiles[i][:, g - g0, b * BANK - c0 : (b + 1) * BANK - c0].bitcast(FP8X4),
+                        rhs_scale=planes[k_off:P, col0 + b * BANK : col0 + (b + 1) * BANK],
+                        start=(g == 0),
+                        stop=(g == GROUPS - 1),
+                    )
+            if g1 == GROUPS:
+                res = keep.tile([P, c1 - c0], F32, name="res%d" % i)
+                for b in range(c0 // BANK, c1 // BANK):
+                    nc.vector.tensor_tensor(
+                        out=res[:, b * BANK - c0 : (b + 1) * BANK - c0],
+                        in0=acc[b][:],
+                        in1=bias_all[:, b * BANK : (b + 1) * BANK],
+                        op=mybir.AluOpType.add,
+                    )
+                nc.sync.dma_start(out=out_rows[:, c0:c1], in_=res[:])

@@ -21,7 +21,7 @@ FLOPS = 2 * P * K * N
 
 G_FULL = 5
 TAIL_RANGES = ((0, 2048, 1), (2048, 3072, 3), (3072, 3584, 3), (3584, 4096, 3))
-SCALES_ON_GPSIMD = False
+SCALES_ON_GPSIMD = True
 
 
 def load_plan():

@@ -20,15 +20,14 @@ N_BANKS = N // BANK
 FLOPS = 2 * P * K * N
 
 G_FULL = 5
-TAIL_RANGES = ((0, 2048, 1), (2048, 3072, 3), (3072, 3584, 3), (3584, 4096, 3))
-SCALES_ON_GPSIMD = True
+TAIL_LOADS = ((5, 6, 0, 2048), (6, 7, 0, 2048), (7, 8, 0, 2048), (5, 8, 2048, 3072), (5, 8, 3072, 3584), (5, 7, 3584, 4096), (7, 8, 3584, 4096))
+SCALE_ORDER = ((0, 2), (0, 3), (1, 2), (1, 3), (0, 0), (0, 1), (1, 0), (1, 1))
+SCALES_ON_GPSIMD = False
 
 
 def load_plan():
     plan = [(g, g + 1, 0, N) for g in range(G_FULL)]
-    for c0, c1, step in TAIL_RANGES:
-        for g in range(G_FULL, GROUPS, step):
-            plan.append((g, min(g + step, GROUPS), c0, c1))
+    plan.extend(TAIL_LOADS)
     return plan
 
 
@@ -58,8 +57,8 @@ def tile_tiledlinear_w_kernel(tc, x_in, weight_words, weight_scales, bias, out):
         make_identity(nc, ident[:])
         nc.scalar.dma_start(out=bias_rows[0:N_BANKS, :], in_=bias.rearrange("(c n) -> c n", c=N_BANKS))
         nc.vector.tensor_copy(out=ident_bf[:], in_=ident[:, 0:N_BANKS])
-        for h in range(2):
-            for q in (0, 1, 2, 3):
+        for h, q in SCALE_ORDER:
+            if True:
                 dst = planes[32 * q : 32 * q + 16, h * N : (h + 1) * N]
                 src = weight_scales[4 * h : 4 * h + 4, 4 * q : 4 * q + 4, :]
                 if SCALES_ON_GPSIMD:

@@ -20,7 +20,7 @@ N_BANKS = N // BANK
 FLOPS = 2 * P * K * N
 
 G_FULL = 5
-TAIL_LOADS = ((5, 6, 0, 2048), (6, 7, 0, 2048), (7, 8, 0, 2048), (5, 8, 2048, 3072), (5, 8, 3072, 3584), (5, 7, 3584, 4096), (7, 8, 3584, 4096))
+TAIL_LOADS = ((5, 6, 0, 2048), (6, 7, 0, 2048), (7, 8, 0, 2048), (5, 6, 2048, 3072), (6, 7, 2048, 3072), (7, 8, 2048, 3072), (5, 7, 3072, 3584), (7, 8, 3072, 3584), (5, 7, 3584, 4096), (7, 8, 3584, 4096))
 SCALE_ORDER = ((0, 2), (0, 3), (1, 2), (1, 3), (0, 0), (0, 1), (1, 0), (1, 1))
 SCALES_ON_GPSIMD = False
 

@@ -13,139 +13,138 @@ FP8X4 = mybir.dt.float8_e4m3fn_x4
 P = 128
 K = 4096
 N = 4096
-K_PASS = 512
+PACK = 4
+K_PASS = P * PACK
 GROUPS = K // K_PASS
 BANK = 512
 N_BANKS = N // BANK
+QUADRANT = 32
+SCALES_PER_QUADRANT = 4
+PLANES_PER_TILE = 4
+LIVE = PLANES_PER_TILE * SCALES_PER_QUADRANT
+PAIRS = K_PASS // 2
 FLOPS = 2 * P * K * N
 
-G_FULL = 5
-TAIL_LOADS = ((5, 6, 0, 2048), (6, 7, 0, 2048), (7, 8, 0, 2048), (5, 6, 2048, 3072), (6, 7, 2048, 3072), (7, 8, 2048, 3072), (5, 7, 3072, 3584), (7, 8, 3072, 3584), (5, 7, 3584, 4096), (7, 8, 3584, 4096))
-SCALE_ORDER = ((0, 2), (0, 3), (1, 2), (1, 3), (0, 0), (0, 1), (1, 0), (1, 1))
-SCALES_ON_GPSIMD = False
-
-
-def load_plan():
-    plan = [(g, g + 1, 0, N) for g in range(G_FULL)]
-    plan.extend(TAIL_LOADS)
-    return plan
+WHOLE_GROUPS = 5
+RANGE_WIDTHS = (2048, 1024, 512, 512)
 
 
 def tile_tiledlinear_w_kernel(tc, x_in, weight_words, weight_scales, bias, out):
     nc = tc.nc
     x_rows = x_in.flatten_outer_dims()
     out_rows = out.flatten_outer_dims()
-    plan = load_plan()
+
+    w_loads = [(g, 0, N) for g in range(WHOLE_GROUPS)]
+    first_column = 0
+    for width in RANGE_WIDTHS:
+        w_loads.extend([(g, first_column, first_column + width) for g in range(WHOLE_GROUPS, GROUPS)])
+        first_column += width
+
     with ExitStack() as stack:
         keep = stack.enter_context(tc.tile_pool(name="keep", bufs=1))
-        banks = stack.enter_context(tc.psum_pool(name="banks", bufs=1))
+        psum = stack.enter_context(tc.psum_pool(name="psum", bufs=1))
         stack.enter_context(tc.manual_schedule())
 
         x_sb = keep.tile([P, K], BF16, name="x_sb", align_bytes=64)
-        grouped = keep.tile([P, K], BF16, name="grouped", align_bytes=64)
-        x_codes = keep.tile([P, K // 4], U32, name="x_codes", align_bytes=64)
-        x_scales = keep.tile([P, K // 4], U8, name="x_scales", align_bytes=64)
-        planes = keep.tile([P, 2 * N], U8, name="planes", align_bytes=64)
+        x_grouped = keep.tile([P, K], BF16, name="x_grouped", align_bytes=64)
+        x_words = keep.tile([P, GROUPS * P], U32, name="x_words", align_bytes=64)
+        x_planes = keep.tile([P, GROUPS * P], U8, name="x_planes", align_bytes=64)
+        w_planes = keep.tile([P, (GROUPS // PLANES_PER_TILE) * N], U8, name="w_planes", align_bytes=64)
         ident = keep.tile([P, P], F32, name="ident")
-        ident_bf = keep.tile([P, N_BANKS], BF16, name="ident_bf")
+        unit_columns = keep.tile([P, N_BANKS], BF16, name="unit_columns")
         bias_rows = keep.tile([P, BANK], BF16, name="bias_rows")
         bias_all = keep.tile([P, N], F32, name="bias_all")
 
         nc.sync.dma_start(out=x_sb[:], in_=x_rows)
-        nc.vector.memset(planes[:].bitcast(I32), 0)
-        nc.vector.memset(bias_rows[:], 0.0)
-        make_identity(nc, ident[:])
-        nc.scalar.dma_start(out=bias_rows[0:N_BANKS, :], in_=bias.rearrange("(c n) -> c n", c=N_BANKS))
-        nc.vector.tensor_copy(out=ident_bf[:], in_=ident[:, 0:N_BANKS])
-        for h, q in SCALE_ORDER:
-            if True:
-                dst = planes[32 * q : 32 * q + 16, h * N : (h + 1) * N]
-                src = weight_scales[4 * h : 4 * h + 4, 4 * q : 4 * q + 4, :]
-                if SCALES_ON_GPSIMD:
-                    nc.gpsimd.dma_start(out=dst.bitcast(F32), in_=src.bitcast(F32))
-                else:
-                    nc.sync.dma_start(out=dst.bitcast(I32), in_=src.bitcast(I32))
-        w_tiles = []
-        for i, (g0, g1, c0, c1) in enumerate(plan):
-            wt = keep.tile([P, g1 - g0, c1 - c0], U32, name="w%d" % i, align_bytes=64)
-            src = weight_words[g0:g1].rearrange("g p n t -> p g (n t)")[:, :, 4 * c0 : 4 * c1]
-            nc.sync.dma_start(out=wt[:].bitcast(I32), in_=src.bitcast(I32))
-            w_tiles.append(wt)
 
-        def bias_matmul(c):
-            bt = banks.tile([P, BANK], F32, name="bias_ps%d" % c, tag="bank%d" % (4 + c % 4))
+        nc.vector.memset(w_planes[:].bitcast(I32), 0)
+        nc.vector.memset(bias_rows[:], 0.0)
+        nc.scalar.dma_start(out=bias_rows[0:N_BANKS, :], in_=bias.rearrange("(c n) -> c n", c=N_BANKS))
+        make_identity(nc, ident[:])
+        nc.vector.tensor_copy(out=unit_columns[:], in_=ident[:, 0:N_BANKS])
+
+        for quadrants in ((2, 3), (0, 1)):
+            for half in range(GROUPS // PLANES_PER_TILE):
+                for quadrant in quadrants:
+                    nc.sync.dma_start(
+                        out=w_planes[
+                            QUADRANT * quadrant : QUADRANT * quadrant + LIVE, half * N : (half + 1) * N
+                        ].bitcast(I32),
+                        in_=weight_scales[
+                            PLANES_PER_TILE * half : PLANES_PER_TILE * (half + 1),
+                            SCALES_PER_QUADRANT * quadrant : SCALES_PER_QUADRANT * (quadrant + 1),
+                            :,
+                        ].bitcast(I32),
+                    )
+
+        w_tiles = []
+        for i, (g, c0, c1) in enumerate(w_loads):
+            w_tile = keep.tile([P, c1 - c0], U32, name="w%d" % i, align_bytes=64)
+            source = weight_words[g].rearrange("p n t -> p (n t)")[:, PACK * c0 : PACK * c1]
+            nc.sync.dma_start(out=w_tile[:].bitcast(I32), in_=source.bitcast(I32))
+            w_tiles.append(w_tile)
+
+        x_pairs = x_sb[:].bitcast(F32)
+        grouped_pairs = x_grouped[:].bitcast(F32)
+        for b in range(GROUPS // 2):
+            flipped = psum.tile([P, 2, 2, P], F32, name="flipped%d" % b, tag="bank%d" % b)
+            for j in range(2):
+                g = 2 * b + j
+                for u in range(2):
+                    nc.tensor.transpose(
+                        out=flipped[:, j, u, :],
+                        in_=x_pairs[:, PAIRS * g + u : PAIRS * (g + 1) : 2],
+                        identity=ident[:],
+                    )
+            target = grouped_pairs[:, BANK * b : BANK * (b + 1)].rearrange("p (j r u) -> p j r u", j=2, u=2)
+            if b % 2 == 0:
+                nc.vector.tensor_copy(out=target, in_=flipped[:].rearrange("p j u r -> p j r u"))
+            else:
+                nc.scalar.copy(out=target, in_=flipped[:].rearrange("p j u r -> p j r u"))
+        for half in range(2):
+            nc.vector.quantize_mx(
+                out=x_words[:, BANK * half : BANK * (half + 1)].bitcast(FP8X4),
+                scales=x_planes[:, BANK * half : BANK * (half + 1)],
+                in_=x_grouped[:, PACK * BANK * half : PACK * BANK * (half + 1)],
+            )
+
+        for c in range(N_BANKS):
+            spread = psum.tile([P, BANK], F32, name="spread%d" % c, tag="bank%d" % (N_BANKS // 2 + c % 4))
             nc.tensor.matmul(
-                out=bt[:],
-                lhsT=ident_bf[:, c : c + 1].to_broadcast([P, P]),
+                out=spread[:],
+                lhsT=unit_columns[:, c : c + 1].to_broadcast([P, P]),
                 rhs=bias_rows[:],
                 start=True,
                 stop=True,
             )
-            return bt
-
-        first = [bias_matmul(c) for c in range(4)]
-        for c in range(4):
-            nc.scalar.copy(out=bias_all[:, c * BANK : (c + 1) * BANK], in_=first[c][:])
-
-        x_words = x_sb[:].bitcast(F32)
-        grouped_words = grouped[:].bitcast(F32)
-        tps = []
-        for b in range(4):
-            tp = banks.tile([P, 2, 2, P], F32, name="tp%d" % b, tag="bank%d" % b)
-            for gi in range(2):
-                g = 2 * b + gi
-                for u in range(2):
-                    nc.tensor.transpose(
-                        out=tp[:, gi, u, :],
-                        in_=x_words[:, 256 * g + u : 256 * (g + 1) : 2],
-                        identity=ident[:],
-                    )
-            tps.append(tp)
-        for b in range(4):
-            dst = grouped_words[:, 512 * b : 512 * (b + 1)].rearrange("p (g r u) -> p g r u", g=2, u=2)
-            src = tps[b][:].rearrange("p g u r -> p g r u")
-            if b < 2:
-                nc.vector.tensor_copy(out=dst, in_=src)
-            else:
-                nc.scalar.copy(out=dst, in_=src)
-        for h in range(2):
-            nc.vector.quantize_mx(
-                out=x_codes[:, 512 * h : 512 * (h + 1)].bitcast(FP8X4),
-                scales=x_scales[:, 512 * h : 512 * (h + 1)],
-                in_=grouped[:, 2048 * h : 2048 * (h + 1)],
-            )
-        second = [bias_matmul(c) for c in range(4, 8)]
-        for c in range(4, 8):
-            dst = bias_all[:, c * BANK : (c + 1) * BANK]
             if c % 2 == 0:
-                nc.scalar.copy(out=dst, in_=second[c - 4][:])
+                nc.scalar.copy(out=bias_all[:, c * BANK : (c + 1) * BANK], in_=spread[:])
             else:
-                nc.vector.tensor_copy(out=dst, in_=second[c - 4][:])
+                nc.vector.tensor_copy(out=bias_all[:, c * BANK : (c + 1) * BANK], in_=spread[:])
 
         acc = {}
-        for i, (g0, g1, c0, c1) in enumerate(plan):
-            for g in range(g0, g1):
-                k_off = 4 * (g % 4)
-                col0 = (g // 4) * N
-                for b in range(c0 // BANK, c1 // BANK):
-                    if g == 0:
-                        acc[b] = banks.tile([P, BANK], F32, name="acc%d" % b, tag="bank%d" % b)
-                    nc.tensor.matmul_mx(
-                        out=acc[b][:],
-                        lhsT=x_codes[:, P * g : P * (g + 1)].bitcast(FP8X4),
-                        lhsT_scale=x_scales[:, P * g : P * (g + 1)],
-                        rhs=w_tiles[i][:, g - g0, b * BANK - c0 : (b + 1) * BANK - c0].bitcast(FP8X4),
-                        rhs_scale=planes[k_off:P, col0 + b * BANK : col0 + (b + 1) * BANK],
-                        start=(g == 0),
-                        stop=(g == GROUPS - 1),
-                    )
-            if g1 == GROUPS:
-                res = keep.tile([P, c1 - c0], F32, name="res%d" % i)
+        for i, (g, c0, c1) in enumerate(w_loads):
+            offset = SCALES_PER_QUADRANT * (g % PLANES_PER_TILE)
+            plane_start = (g // PLANES_PER_TILE) * N
+            for b in range(c0 // BANK, c1 // BANK):
+                if g == 0:
+                    acc[b] = psum.tile([P, BANK], F32, name="acc%d" % b, tag="bank%d" % b)
+                nc.tensor.matmul_mx(
+                    out=acc[b][:],
+                    lhsT=x_words[:, P * g : P * (g + 1)].bitcast(FP8X4),
+                    lhsT_scale=x_planes[:, P * g : P * (g + 1)],
+                    rhs=w_tiles[i][:, b * BANK - c0 : (b + 1) * BANK - c0].bitcast(FP8X4),
+                    rhs_scale=w_planes[offset:P, plane_start + b * BANK : plane_start + (b + 1) * BANK],
+                    start=(g == 0),
+                    stop=(g == GROUPS - 1),
+                )
+            if g == GROUPS - 1:
+                result = keep.tile([P, c1 - c0], F32, name="result%d" % i)
                 for b in range(c0 // BANK, c1 // BANK):
                     nc.vector.tensor_tensor(
-                        out=res[:, b * BANK - c0 : (b + 1) * BANK - c0],
+                        out=result[:, b * BANK - c0 : (b + 1) * BANK - c0],
                         in0=acc[b][:],
                         in1=bias_all[:, b * BANK : (b + 1) * BANK],
                         op=mybir.AluOpType.add,
                     )
-                nc.sync.dma_start(out=out_rows[:, c0:c1], in_=res[:])
+                nc.sync.dma_start(out=out_rows[:, c0:c1], in_=result[:])

@@ -25,8 +25,9 @@ LIVE = PLANES_PER_TILE * SCALES_PER_QUADRANT
 PAIRS = K_PASS // 2
 FLOPS = 2 * P * K * N
 
-WHOLE_GROUPS = 5
+WHOLE_GROUPS = 6
 RANGE_WIDTHS = (2048, 1024, 512, 512)
+STORE_WIDTH = 1024
 
 
 def tile_tiledlinear_w_kernel(tc, x_in, weight_words, weight_scales, bias, out):
@@ -139,12 +140,14 @@ def tile_tiledlinear_w_kernel(tc, x_in, weight_words, weight_scales, bias, out):
                     stop=(g == GROUPS - 1),
                 )
             if g == GROUPS - 1:
-                result = keep.tile([P, c1 - c0], F32, name="result%d" % i)
-                for b in range(c0 // BANK, c1 // BANK):
-                    nc.vector.tensor_tensor(
-                        out=result[:, b * BANK - c0 : (b + 1) * BANK - c0],
-                        in0=acc[b][:],
-                        in1=bias_all[:, b * BANK : (b + 1) * BANK],
-                        op=mybir.AluOpType.add,
-                    )
-                nc.sync.dma_start(out=out_rows[:, c0:c1], in_=result[:])
+                for s0 in range(c0, c1, STORE_WIDTH):
+                    s1 = min(s0 + STORE_WIDTH, c1)
+                    result = keep.tile([P, s1 - s0], F32, name="result%d" % s0)
+                    for b in range(s0 // BANK, s1 // BANK):
+                        nc.vector.tensor_tensor(
+                            out=result[:, b * BANK - s0 : (b + 1) * BANK - s0],
+                            in0=acc[b][:],
+                            in1=bias_all[:, b * BANK : (b + 1) * BANK],
+                            op=mybir.AluOpType.add,
+                        )
+                    nc.sync.dma_start(out=out_rows[:, s0:s1], in_=result[:])

@@ -58,25 +58,40 @@ def tile_tiledlinear_w_kernel(tc, x_in, weight_words, weight_scales, bias, out):
 
         nc.sync.dma_start(out=x_sb[:], in_=x_rows)
 
-        nc.vector.memset(w_planes[:].bitcast(I32), 0)
+        for half in range(2):
+            nc.vector.memset(w_planes[:, half * N : (half + 1) * N].bitcast(I32), 0)
         nc.vector.memset(bias_rows[:], 0.0)
         nc.scalar.dma_start(out=bias_rows[0:N_BANKS, :], in_=bias.rearrange("(c n) -> c n", c=N_BANKS))
         make_identity(nc, ident[:])
         nc.vector.tensor_copy(out=unit_columns[:], in_=ident[:, 0:N_BANKS])
 
-        for quadrants in ((2, 3), (0, 1)):
-            for half in range(GROUPS // PLANES_PER_TILE):
-                for quadrant in quadrants:
-                    nc.sync.dma_start(
-                        out=w_planes[
-                            QUADRANT * quadrant : QUADRANT * quadrant + LIVE, half * N : (half + 1) * N
-                        ].bitcast(I32),
-                        in_=weight_scales[
-                            PLANES_PER_TILE * half : PLANES_PER_TILE * (half + 1),
-                            SCALES_PER_QUADRANT * quadrant : SCALES_PER_QUADRANT * (quadrant + 1),
-                            :,
-                        ].bitcast(I32),
-                    )
+        turn = keep.tile([P, 2, QUADRANT], F32, name="turn")
+
+        def planes_of(quadrant, half):
+            p0 = QUADRANT * quadrant
+            return (
+                w_planes[p0 : p0 + LIVE, half * N : (half + 1) * N],
+                weight_scales[
+                    PLANES_PER_TILE * half : PLANES_PER_TILE * (half + 1),
+                    SCALES_PER_QUADRANT * quadrant : SCALES_PER_QUADRANT * (quadrant + 1),
+                    :,
+                ],
+            )
+
+        def take_turns(engines):
+            nc.gpsimd.dma_start(
+                out=turn[0:engines, :, 0:16],
+                in_=weight_scales[0, 0:engines, 0:128].bitcast(F32).rearrange("p (s c) -> p s c", s=2),
+            )
+
+        take_turns(8)
+        for half, quadrant in ((0, 2), (0, 3), (1, 2), (1, 3)):
+            target, source = planes_of(quadrant, half)
+            nc.gpsimd.dma_start(out=target.bitcast(F32), in_=source.bitcast(F32))
+            take_turns(4 if (half, quadrant) == (1, 3) else 12)
+        for half, quadrant in ((0, 0), (0, 1), (1, 0), (1, 1)):
+            target, source = planes_of(quadrant, half)
+            nc.sync.dma_start(out=target.bitcast(I32), in_=source.bitcast(I32))
 
         w_tiles = []
         for i, (g, c0, c1) in enumerate(w_loads):

from contextlib import ExitStack

import concourse.mybir as mybir
from concourse.masks import make_identity

F32 = mybir.dt.float32
BF16 = mybir.dt.bfloat16
U32 = mybir.dt.uint32
U8 = mybir.dt.uint8
I32 = mybir.dt.int32
FP8X4 = mybir.dt.float8_e4m3fn_x4

P = 128
K = 4096
N = 4096
PACK = 4
K_PASS = P * PACK
GROUPS = K // K_PASS
BANK = 512
N_BANKS = N // BANK
QUADRANT = 32
SCALES_PER_QUADRANT = 4
PLANES_PER_TILE = 4
LIVE = PLANES_PER_TILE * SCALES_PER_QUADRANT
PAIRS = K_PASS // 2
FLOPS = 2 * P * K * N

WHOLE_GROUPS = 6
RANGE_WIDTHS = (2048, 1024, 512, 512)
STORE_WIDTH = 1024


def tile_tiledlinear_w_kernel(tc, x_in, weight_words, weight_scales, bias, out):
    nc = tc.nc
    x_rows = x_in.flatten_outer_dims()
    out_rows = out.flatten_outer_dims()

    w_loads = [(g, 0, N) for g in range(WHOLE_GROUPS)]
    first_column = 0
    for width in RANGE_WIDTHS:
        w_loads.extend([(g, first_column, first_column + width) for g in range(WHOLE_GROUPS, GROUPS)])
        first_column += width

    with ExitStack() as stack:
        keep = stack.enter_context(tc.tile_pool(name="keep", bufs=1))
        psum = stack.enter_context(tc.psum_pool(name="psum", bufs=1))
        stack.enter_context(tc.manual_schedule())

        x_sb = keep.tile([P, K], BF16, name="x_sb", align_bytes=64)
        x_grouped = keep.tile([P, K], BF16, name="x_grouped", align_bytes=64)
        x_words = keep.tile([P, GROUPS * P], U32, name="x_words", align_bytes=64)
        x_planes = keep.tile([P, GROUPS * P], U8, name="x_planes", align_bytes=64)
        w_planes = keep.tile([P, (GROUPS // PLANES_PER_TILE) * N], U8, name="w_planes", align_bytes=64)
        ident = keep.tile([P, P], F32, name="ident")
        unit_columns = keep.tile([P, N_BANKS], BF16, name="unit_columns")
        bias_rows = keep.tile([P, BANK], BF16, name="bias_rows")
        bias_all = keep.tile([P, N], F32, name="bias_all")

        nc.sync.dma_start(out=x_sb[:], in_=x_rows)

        for half in range(2):
            nc.vector.memset(w_planes[:, half * N : (half + 1) * N].bitcast(I32), 0)
        nc.vector.memset(bias_rows[:], 0.0)
        nc.scalar.dma_start(out=bias_rows[0:N_BANKS, :], in_=bias.rearrange("(c n) -> c n", c=N_BANKS))
        make_identity(nc, ident[:])
        nc.vector.tensor_copy(out=unit_columns[:], in_=ident[:, 0:N_BANKS])

        turn = keep.tile([P, 2, QUADRANT], F32, name="turn")

        def planes_of(quadrant, half):
            p0 = QUADRANT * quadrant
            return (
                w_planes[p0 : p0 + LIVE, half * N : (half + 1) * N],
                weight_scales[
                    PLANES_PER_TILE * half : PLANES_PER_TILE * (half + 1),
                    SCALES_PER_QUADRANT * quadrant : SCALES_PER_QUADRANT * (quadrant + 1),
                    :,
                ],
            )

        def take_turns(engines):
            nc.gpsimd.dma_start(
                out=turn[0:engines, :, 0:16],
                in_=weight_scales[0, 0:engines, 0:128].bitcast(F32).rearrange("p (s c) -> p s c", s=2),
            )

        take_turns(8)
        for half, quadrant in ((0, 2), (0, 3), (1, 2), (1, 3)):
            target, source = planes_of(quadrant, half)
            nc.gpsimd.dma_start(out=target.bitcast(F32), in_=source.bitcast(F32))
            take_turns(4 if (half, quadrant) == (1, 3) else 12)
        for half, quadrant in ((0, 0), (0, 1), (1, 0), (1, 1)):
            target, source = planes_of(quadrant, half)
            nc.sync.dma_start(out=target.bitcast(I32), in_=source.bitcast(I32))

        w_tiles = []
        for i, (g, c0, c1) in enumerate(w_loads):
            w_tile = keep.tile([P, c1 - c0], U32, name="w%d" % i, align_bytes=64)
            source = weight_words[g].rearrange("p n t -> p (n t)")[:, PACK * c0 : PACK * c1]
            nc.sync.dma_start(out=w_tile[:].bitcast(I32), in_=source.bitcast(I32))
            w_tiles.append(w_tile)

        x_pairs = x_sb[:].bitcast(F32)
        grouped_pairs = x_grouped[:].bitcast(F32)
        for b in range(GROUPS // 2):
            flipped = psum.tile([P, 2, 2, P], F32, name="flipped%d" % b, tag="bank%d" % b)
            for j in range(2):
                g = 2 * b + j
                for u in range(2):
                    nc.tensor.transpose(
                        out=flipped[:, j, u, :],
                        in_=x_pairs[:, PAIRS * g + u : PAIRS * (g + 1) : 2],
                        identity=ident[:],
                    )
            target = grouped_pairs[:, BANK * b : BANK * (b + 1)].rearrange("p (j r u) -> p j r u", j=2, u=2)
            if b % 2 == 0:
                nc.vector.tensor_copy(out=target, in_=flipped[:].rearrange("p j u r -> p j r u"))
            else:
                nc.scalar.copy(out=target, in_=flipped[:].rearrange("p j u r -> p j r u"))
        for half in range(2):
            nc.vector.quantize_mx(
                out=x_words[:, BANK * half : BANK * (half + 1)].bitcast(FP8X4),
                scales=x_planes[:, BANK * half : BANK * (half + 1)],
                in_=x_grouped[:, PACK * BANK * half : PACK * BANK * (half + 1)],
            )

        for c in range(N_BANKS):
            spread = psum.tile([P, BANK], F32, name="spread%d" % c, tag="bank%d" % (N_BANKS // 2 + c % 4))
            nc.tensor.matmul(
                out=spread[:],
                lhsT=unit_columns[:, c : c + 1].to_broadcast([P, P]),
                rhs=bias_rows[:],
                start=True,
                stop=True,
            )
            if c % 2 == 0:
                nc.scalar.copy(out=bias_all[:, c * BANK : (c + 1) * BANK], in_=spread[:])
            else:
                nc.vector.tensor_copy(out=bias_all[:, c * BANK : (c + 1) * BANK], in_=spread[:])

        acc = {}
        for i, (g, c0, c1) in enumerate(w_loads):
            offset = SCALES_PER_QUADRANT * (g % PLANES_PER_TILE)
            plane_start = (g // PLANES_PER_TILE) * N
            for b in range(c0 // BANK, c1 // BANK):
                if g == 0:
                    acc[b] = psum.tile([P, BANK], F32, name="acc%d" % b, tag="bank%d" % b)
                nc.tensor.matmul_mx(
                    out=acc[b][:],
                    lhsT=x_words[:, P * g : P * (g + 1)].bitcast(FP8X4),
                    lhsT_scale=x_planes[:, P * g : P * (g + 1)],
                    rhs=w_tiles[i][:, b * BANK - c0 : (b + 1) * BANK - c0].bitcast(FP8X4),
                    rhs_scale=w_planes[offset:P, plane_start + b * BANK : plane_start + (b + 1) * BANK],
                    start=(g == 0),
                    stop=(g == GROUPS - 1),
                )
            if g == GROUPS - 1:
                for s0 in range(c0, c1, STORE_WIDTH):
                    s1 = min(s0 + STORE_WIDTH, c1)
                    result = keep.tile([P, s1 - s0], F32, name="result%d" % s0)
                    for b in range(s0 // BANK, s1 // BANK):
                        nc.vector.tensor_tensor(
                            out=result[:, b * BANK - s0 : (b + 1) * BANK - s0],
                            in0=acc[b][:],
                            in1=bias_all[:, b * BANK : (b + 1) * BANK],
                            op=mybir.AluOpType.add,
                        )
                    nc.sync.dma_start(out=out_rows[:, s0:s1], in_=result[:])
